import numpy as np
import ml_dtypes


def mxq(x, axis, fmt="e4m3"):
    dtype, down = {"e4m3": (ml_dtypes.float8_e4m3fn, 7), "e5m2": (ml_dtypes.float8_e5m2, 14)}[fmt]
    v = np.moveaxis(np.asarray(x, np.float32).astype(ml_dtypes.bfloat16).astype(np.float64), axis, -1)
    blocks = v.reshape(v.shape[:-1] + (-1, 32))
    amax = np.abs(blocks).max(-1, keepdims=True)
    byte = np.maximum(np.where(amax > 0, np.frexp(amax)[1] - 1 + 127, 0) - down, 1)
    scale = np.exp2(byte - 127.0)
    codes = (blocks / scale).astype(np.float32).astype(dtype).astype(np.float64)
    return np.moveaxis((codes * scale).reshape(v.shape), -1, axis)


WIDE = False


def mx_kscale(k):
    if not WIDE:
        return np.ones(k)
    levels = np.array([10, -10, 5, -5, 0])
    if k % 512:
        return np.exp2(np.random.permutation(np.resize(levels, k // 32))).repeat(32)
    a = np.empty((k // 512, 16))
    for p in range(k // 512):
        a[p, :8] = np.random.permutation(np.resize(levels, 8))
        for g in range(8):
            far = levels[np.abs(levels - a[p, g]) >= 10]
            a[p, g + 8] = far[np.random.randint(len(far))]
    return np.exp2(a.ravel()).repeat(32)


BF16 = ml_dtypes.bfloat16


def bf(x):
    return np.asarray(x, np.float32).astype(BF16)


def f64(x):
    return np.asarray(x).astype(np.float64)


B, C, P, NH, NW = 4, 4, 16, 16, 16
D = C * P * P
QK_SCALE = 1.0


def rel_bias(p):
    i = np.arange(p, dtype=np.float64)
    down = np.exp(-i / (p / 2))[:, None] * np.ones((1, p))
    right = down.T
    br = np.exp(-(i[:, None] + i[None, :]) / (p / 2))
    return np.stack([
        np.rot90(br, 2), np.flip(down, 0), np.rot90(br, 1),
        np.flip(right, 1), np.ones((p, p)), right,
        np.rot90(br, 3), down, br,
    ], axis=0)


def setup_inputs():
    s = mx_kscale(D)
    sx = np.tile(s.reshape(C, P, P), (1, NH, NW))
    return {"x": bf(np.random.standard_normal((B, C, NH * P, NW * P)) * sx),
            "W_qkv": bf(np.random.standard_normal((3 * D, D)) / np.sqrt(D) / s),
            "b_qkv": bf(np.random.standard_normal(3 * D) * 0.5)}


def reference(x, W_qkv, b_qkv):
    p, c = P, C
    b, _, h, w = x.shape
    nh, nw = h // p, w // p
    feat = f64(x).reshape(b, c, nh, p, nw, p).transpose(0, 2, 4, 1, 3, 5).reshape(b, nh, nw, c * p * p)
    y = mxq(feat, 3, "e4m3") @ mxq(f64(W_qkv), 1, "e4m3").T
    qkv = np.pad(y, ((0, 0), (1, 1), (1, 1), (0, 0))) + f64(b_qkv)
    qkv = qkv.reshape(b, nh + 2, nw + 2, 3, c, p, p)
    core_q = qkv[:, 1:nh + 1, 1:nw + 1, 0] * QK_SCALE
    k = np.stack([qkv[:, di:di + nh, dj:dj + nw, 1] for di in range(3) for dj in range(3)], axis=3)
    v = np.stack([qkv[:, di:di + nh, dj:dj + nw, 2] for di in range(3) for dj in range(3)], axis=3)
    bias = rel_bias(p)
    attn = core_q[:, :, :, None] * k * bias[:, None]
    out = np.sum(attn * v, axis=3)
    return out.transpose(0, 3, 1, 4, 2, 5).reshape(b, c, nh * p, nw * p)

@@ -1,0 +1,382 @@
+from contextlib import ExitStack
+
+import concourse.mybir as mybir
+from concourse.masks import make_identity
+
+F32 = mybir.dt.float32
+BF16 = mybir.dt.bfloat16
+U32 = mybir.dt.uint32
+U8 = mybir.dt.uint8
+I32 = mybir.dt.int32
+FP8X4 = mybir.dt.float8_e4m3fn_x4
+ALU = mybir.AluOpType
+ACT = mybir.ActivationFunctionType
+
+FLOPS = 2 * 1024 * 1024 * 3072
+
+P = 128
+NCHUNK = 8
+NPATCH = 1024
+BANK = 512
+YJ = 64
+TROW = 80
+GP_J = 12
+
+
+def tile_attentionconv_kernel(tc, x, W_qkv, b_qkv, out):
+    nc = tc.nc
+    with ExitStack() as ctx:
+        const = ctx.enter_context(tc.tile_pool(name="const", bufs=1))
+        xpool = ctx.enter_context(tc.tile_pool(name="xpool", bufs=1))
+        wnat = ctx.enter_context(tc.tile_pool(name="wnat", bufs=NCHUNK))
+        work3 = ctx.enter_context(tc.tile_pool(name="work3", bufs=3))
+        work2 = ctx.enter_context(tc.tile_pool(name="work2", bufs=2))
+        work1 = ctx.enter_context(tc.tile_pool(name="work1", bufs=1))
+        ps_mx = ctx.enter_context(tc.psum_pool(name="ps_mx", bufs=2))
+        ps_tp = ctx.enter_context(tc.psum_pool(name="ps_tp", bufs=2))
+        ctx.enter_context(tc.manual_schedule())
+
+        vcopy = nc.vector.tensor_copy
+        scopy = nc.scalar.copy
+
+        def bank(tag):
+            pool = ps_tp if tag == "tp" else ps_mx
+            return pool.tile([P, 4, P], F32, name="bk", tag=tag)
+
+        b_rows = const.tile([24, P], BF16, name="b_rows")
+        nc.sync.dma_start(out=b_rows[:], in_=b_qkv.rearrange("(t p) -> t p", p=P))
+        x_rows = x.rearrange("b (g l) (i r) w -> l i (b g) (r w)", l=2, r=16)
+        w_view = W_qkv.rearrange("(s c p) k -> c p s k", s=3, c=NCHUNK, p=P)
+        xn = [xpool.tile([P, 4096], BF16, name="xn%d" % h) for h in range(2)]
+        wn = [wnat.tile([P, 3, 1024], BF16, name="wn", tag="wn") for c in range(NCHUNK)]
+
+        def load_x(h):
+            nc.sync.dma_start(out=xn[h][:], in_=x_rows[h])
+
+        def load_kv(c):
+            nc.sync.dma_start(out=wn[c][:, 1:3, :], in_=w_view[c][:, 1:3, :])
+
+        def load_q(c):
+            nc.sync.dma_start(out=wn[c][:, 0:1, :], in_=w_view[c][:, 0:1, :])
+
+        load_x(0)
+        load_x(1)
+        load_kv(0)
+        load_kv(1)
+        load_q(0)
+        for c in range(2, NCHUNK):
+            load_kv(c)
+            load_q(c - 1)
+        load_q(NCHUNK - 1)
+
+        ident = const.tile([P, P], F32, name="ident")
+        make_identity(nc, ident[:])
+        pidx = const.tile([P, 1], I32, name="pidx")
+        nc.gpsimd.iota(pidx[:], pattern=[[0, 1]], base=0, channel_multiplier=1)
+        ones = const.tile([P, P], F32, name="ones")
+        nc.gpsimd.memset(ones[:], 1.0)
+        s_i = const.tile([P, 1], I32, name="s_i")
+        nc.vector.tensor_single_scalar(out=s_i[:], in_=pidx[:], scalar=15, op=ALU.bitwise_and)
+        r_i = const.tile([P, 1], I32, name="r_i")
+        nc.vector.tensor_single_scalar(out=r_i[:], in_=pidx[:], scalar=4, op=ALU.logical_shift_right)
+        s_f = const.tile([P, 1], F32, name="s_f")
+        vcopy(out=s_f[:], in_=s_i[:])
+        r_f = const.tile([P, 1], F32, name="r_f")
+        vcopy(out=r_f[:], in_=r_i[:])
+        tab = const.tile([P, 8], F32, name="tab")
+        nc.scalar.activation(out=tab[:, 0:1], in_=s_f[:], func=ACT.Exp, scale=0.125, bias=-1.875)
+        nc.scalar.activation(out=tab[:, 1:2], in_=s_f[:], func=ACT.Exp, scale=-0.125)
+        for rh in range(2):
+            nc.scalar.activation(
+                out=tab[:, 2 + rh : 3 + rh], in_=r_f[:], func=ACT.Exp, scale=0.125, bias=(8.0 * rh - 15.0) / 8.0
+            )
+            nc.scalar.activation(
+                out=tab[:, 4 + rh : 5 + rh], in_=r_f[:], func=ACT.Exp, scale=-0.125, bias=-1.0 * rh
+            )
+        b_rows_f = const.tile([P, P], F32, name="b_rows_f")
+        nc.vector.memset(b_rows_f[:], 0.0)
+        hs = const.tile([P, 1], F32, name="hs")
+        nc.vector.scalar_tensor_tensor(
+            out=hs[:], in0=tab[:, 0:1], scalar=1.0, in1=tab[:, 1:2], op0=ALU.add, op1=ALU.add
+        )
+        vcopy(out=b_rows_f[0:24, :], in_=b_rows[:])
+        b_ps = bank("tp")
+        nc.tensor.transpose(out=b_ps[:, 0, :], in_=b_rows_f[:], identity=ident[:])
+        bias = const.tile([P, 24], F32, name="bias")
+        vcopy(out=bias[:], in_=b_ps[:, 0, 0:24])
+        cb = const.tile([P, NCHUNK], F32, name="cb")
+        nc.vector.tensor_mul(out=cb[:], in0=bias[:, 8:16], in1=bias[:, 16:24])
+        cbh = const.tile([P, NCHUNK], F32, name="cbh")
+        nc.vector.tensor_scalar_mul(out=cbh[:], in0=cb[:], scalar1=hs[:, 0:1])
+
+        xr = xpool.tile([P, 4096], F32, name="xr")
+        xg = [xpool.tile([P, 4096], BF16, name="xg%d" % g, align_bytes=64) for g in range(2)]
+        xc = [xpool.tile([P, NPATCH], U32, name="xc%d" % g, align_bytes=64) for g in range(2)]
+        xs = [xpool.tile([P, NPATCH], U8, name="xs%d" % g, align_bytes=64) for g in range(2)]
+
+        def x_reorder(l, q, copy):
+            src = xn[l][:].bitcast(F32).rearrange("p (r j s u) -> p u j r s", r=16, j=16, s=4, u=2)
+            dst = xr[:].rearrange("p (j u l r s) -> p u l j r s", j=16, u=2, l=2, r=16, s=4)
+            for u in range(2):
+                copy(out=dst[:, u, l, 4 * q : 4 * q + 4], in_=src[:, u, 4 * q : 4 * q + 4])
+
+        def x_bank(jp, tag, copy):
+            t = bank(tag)
+            for ju in range(4):
+                c0 = (4 * jp + ju) * P
+                nc.tensor.transpose(out=t[:, ju, :], in_=xr[:, c0 : c0 + P], identity=ident[:])
+            src = t[:].rearrange("p (j u) (n g) -> p g j n u", j=2, u=2, n=YJ, g=2)
+            for g in range(2):
+                dst = xg[g][:].bitcast(F32).rearrange("p (j n u) -> p j n u", j=16, n=YJ, u=2)
+                copy(out=dst[:, 2 * jp : 2 * jp + 2], in_=src[:, g])
+
+        def x_quant(half, g):
+            nc.vector.quantize_mx(
+                out=xc[g][:, half * BANK : (half + 1) * BANK].bitcast(FP8X4),
+                scales=xs[g][:, half * BANK : (half + 1) * BANK],
+                in_=xg[g][:, half * 4 * BANK : (half + 1) * 4 * BANK],
+            )
+
+        wg_kv = {}
+        wg_q = {}
+        wc_kv = {}
+        ws_kv = {}
+        wc_q = {}
+        ws_q = {}
+
+        def w_bank(c, section, dst):
+            wt = bank("tp")
+            words = wn[c][:, section, :].bitcast(F32)
+            for chn in range(4):
+                g, u = divmod(chn, 2)
+                nc.tensor.transpose(
+                    out=wt[:, chn, :], in_=words[:, 256 * g + u : 256 * (g + 1) : 2], identity=ident[:]
+                )
+            scopy(out=dst, in_=wt[:].rearrange("p (g u) o -> p g o u", g=2, u=2))
+
+        def w_transpose_kv(c):
+            wg_kv[c] = work2.tile([P, 2048], BF16, name="wgkv", tag="wgkv", align_bytes=64)
+            v = wg_kv[c][:].bitcast(F32).rearrange("p (t g o u) -> p t g o u", t=2, g=2, o=P, u=2)
+            w_bank(c, 1, v[:, 0])
+            w_bank(c, 2, v[:, 1])
+
+        def w_transpose_q(c):
+            wg_q[c] = work2.tile([P, 1024], BF16, name="wgq", tag="wgq", align_bytes=64)
+            w_bank(c, 0, wg_q[c][:].bitcast(F32).rearrange("p (g o u) -> p g o u", g=2, o=P, u=2))
+
+        def w_quant_kv(c):
+            wc_kv[c] = work3.tile([P, 512], U32, name="wckv", tag="wckv", align_bytes=64)
+            ws_kv[c] = work3.tile([P, 512], U8, name="wskv", tag="wskv", align_bytes=64)
+            nc.vector.quantize_mx(out=wc_kv[c][:].bitcast(FP8X4), scales=ws_kv[c][:], in_=wg_kv[c][:])
+
+        def w_quant_q(c):
+            wc_q[c] = work3.tile([P, 256], U32, name="wcq", tag="wcq", align_bytes=64)
+            ws_q[c] = work3.tile([P, 256], U8, name="wsq", tag="wsq", align_bytes=64)
+            nc.vector.quantize_mx(out=wc_q[c][:].bitcast(FP8X4), scales=ws_q[c][:], in_=wg_q[c][:])
+
+        def mx(codes, scales, first, half, tag):
+            acc = ps_mx.tile([P, BANK], F32, name="acc", tag=tag)
+            pats = slice(half * BANK, (half + 1) * BANK)
+            for g in range(2):
+                cols = slice(first + g * P, first + (g + 1) * P)
+                nc.tensor.matmul_mx(
+                    out=acc[:],
+                    lhsT=codes[:, cols].bitcast(FP8X4),
+                    lhsT_scale=scales[:, cols],
+                    rhs=xc[g][:, pats].bitcast(FP8X4),
+                    rhs_scale=xs[g][:, pats],
+                    start=(g == 0),
+                    stop=(g == 1),
+                )
+            return acc
+
+        ks = {}
+        v_ps = {}
+        q_ps = {}
+        kv = {}
+        tt = {}
+        pt = {}
+        qt = {}
+        zt = {}
+        ut = {}
+        o_tiles = {}
+        os_tiles = {}
+
+        def borders(c):
+            kv[c] = work2.tile([P, 18, YJ], F32, name="kv", tag="kv")
+            nc.scalar.activation(
+                out=kv[c][:, 0:18:17, :],
+                in_=ones[:].rearrange("p (a y) -> p a y", a=2),
+                func=ACT.Copy,
+                scale=cb[:, c : c + 1],
+            )
+            tt[c] = work3.tile([P, 16, TROW], F32, name="tt", tag="tt")
+            nc.scalar.activation(
+                out=tt[c][:].rearrange("p j (l f) -> p j l f", f=4)[:, :, 1:19:17, :],
+                in_=ones[:].rearrange("p (j l f) -> p j l f", j=16, l=2, f=4),
+                func=ACT.Copy,
+                scale=cbh[:, c : c + 1],
+            )
+
+        def front(c, half):
+            if half == 0:
+                ks[c] = work2.tile([P, NPATCH], F32, name="ks", tag="ks")
+            k_ps = mx(wc_kv[c], ws_kv[c], 0, half, "acc0")
+            v_ps[(c, half)] = mx(wc_kv[c], ws_kv[c], 256, half, "acc1")
+            nc.scalar.activation(
+                out=ks[c][:, half * BANK : (half + 1) * BANK], in_=k_ps[:], func=ACT.Identity,
+                bias=bias[:, 8 + c : 9 + c], scale=1.0,
+            )
+
+        def mx_q(c):
+            for half in range(2):
+                q_ps[(c, half)] = mx(wc_q[c], ws_q[c], 0, half, "acc2")
+
+        def stt(o, a, s, b, op0, op1):
+            nc.vector.scalar_tensor_tensor(out=o, in0=a, scalar=s, in1=b, op0=op0, op1=op1)
+
+        def st_k(c, half):
+            flat = kv[c][:].rearrange("p a y -> p (a y)")
+            stt(
+                flat[:, YJ + half * BANK : YJ + (half + 1) * BANK], v_ps[(c, half)][:], bias[:, 16 + c : 17 + c],
+                ks[c][:, half * BANK : (half + 1) * BANK], ALU.add, ALU.mult,
+            )
+
+        def st_h1(c):
+            flat = kv[c][:].rearrange("p a y -> p (a y)")
+            pt[c] = work1.tile([P, 16, YJ], F32, name="pt", tag="pt")
+            stt(
+                pt[c][:].rearrange("p j y -> p (j y)"), flat[:, 0:NPATCH], tab[:, 0:1], flat[:, YJ : YJ + NPATCH],
+                ALU.mult, ALU.add,
+            )
+
+        def st_h2(c):
+            stt(tt[c][:, :, 8:72], kv[c][:, 2:18, :], tab[:, 1:2], pt[c][:], ALU.mult, ALU.add)
+
+        def st_v1(c):
+            rh = c % 2
+            qt[c] = work2.tile([P, 16, YJ], F32, name="qt", tag="qt")
+            ut[c] = work2.tile([P, 16, YJ], F32, name="ut", tag="ut")
+            stt(qt[c][:], tt[c][:, :, 4:68], tab[:, 2 + rh : 3 + rh], tt[c][:, :, 8:72], ALU.mult, ALU.add)
+
+        def st_z(c):
+            rh = c % 2
+            zt[c] = work2.tile([P, GP_J, YJ], F32, name="zt", tag="zt")
+            nc.scalar.activation(
+                out=zt[c][:], in_=tt[c][:, 0:GP_J, 12:76], func=ACT.Copy, scale=tab[:, 4 + rh : 5 + rh]
+            )
+
+        def st_g(c):
+            nc.gpsimd.tensor_tensor(out=ut[c][:, 0:GP_J, :], in0=qt[c][:, 0:GP_J, :], in1=zt[c][:], op=ALU.add)
+
+        def st_v2(c, js):
+            rh = c % 2
+            stt(ut[c][:, js, :], tt[c][:, js, 12:76], tab[:, 4 + rh : 5 + rh], qt[c][:, js, :], ALU.mult, ALU.add)
+
+        def st_f(c, half):
+            ch = c // 2
+            rh = c % 2
+            if ch not in o_tiles:
+                o_tiles[ch] = work2.tile([P, 2048], F32, name="ot", tag="ot")
+            o_v = o_tiles[ch][:].rearrange("p (n a b) -> p n a b", a=2, b=4)
+            stt(
+                o_v[:, half * P : (half + 1) * P, rh, :],
+                q_ps[(c, half)][:].rearrange("p (n b) -> p n b", b=4),
+                bias[:, c : c + 1],
+                ut[c][:].rearrange("p j (i b) -> p (j i) b", b=4)[:, half * P : (half + 1) * P, :],
+                ALU.add, ALU.mult,
+            )
+
+        def out_bank(ch, q, copy, tag):
+            if ch not in os_tiles:
+                os_tiles[ch] = work2.tile([P, 8, 16, 16], F32, name="os_t", tag="os")
+            tp = bank(tag)
+            for jj in range(4):
+                j = 4 * q + jj
+                nc.tensor.transpose(out=tp[:, jj, :], in_=o_tiles[ch][:, j * P : (j + 1) * P], identity=ident[:])
+            copy(
+                out=os_tiles[ch][:, :, 4 * q : 4 * q + 4, :],
+                in_=tp[:].rearrange("p j (r s) -> p r j s", r=8, s=16),
+            )
+
+        def out_store(ch):
+            os_flat = os_tiles[ch][:].rearrange("p r j s -> p (r j s)")
+            for b in range(4):
+                nc.sync.dma_start(
+                    out=out[b, ch].rearrange("(m r) w -> m (r w)", r=8), in_=os_flat[b : b + 125 : 4, :]
+                )
+
+        borders(0)
+        for l in range(2):
+            for q in range(4):
+                x_reorder(l, q, scopy if q == 1 else vcopy)
+        x_bank(0, "acc0", vcopy)
+        x_bank(1, "acc0", scopy)
+        x_bank(2, "acc1", vcopy)
+        x_bank(3, "acc1", scopy)
+        w_transpose_kv(0)
+        x_bank(4, "acc2", vcopy)
+        x_bank(5, "acc2", scopy)
+        w_quant_kv(0)
+        x_quant(0, 0)
+        x_quant(0, 1)
+        x_bank(6, "acc0", scopy)
+        x_bank(7, "acc1", scopy)
+        w_transpose_kv(1)
+        front(0, 0)
+        x_quant(1, 0)
+        x_quant(1, 1)
+        front(0, 1)
+        w_quant_kv(1)
+        w_transpose_kv(2)
+        w_transpose_q(0)
+
+        last = NCHUNK - 1
+        for p in range(NCHUNK + 2):
+            if p <= last:
+                st_k(p, 0)
+                st_k(p, 1)
+            if 1 <= p <= last and GP_J > 0:
+                st_g(p - 1)
+            if 2 <= p <= last + 1:
+                st_f(p - 2, 0)
+                st_f(p - 2, 1)
+            if p == last + 2:
+                st_f(last, 0)
+                out_bank(3, 0, scopy, "tp")
+                out_bank(3, 1, scopy, "tp")
+                st_f(last, 1)
+                out_bank(3, 2, vcopy, "acc0")
+                out_bank(3, 3, scopy, "acc1")
+                out_store(3)
+            if p + 1 <= last:
+                borders(p + 1)
+                front(p + 1, 0)
+                front(p + 1, 1)
+            if 1 <= p <= last + 1:
+                mx_q(p - 1)
+            if p <= last:
+                st_h1(p)
+            if 1 <= p <= last and GP_J < 16:
+                st_v2(p - 1, slice(GP_J, 16))
+            if p == last + 1:
+                st_v2(last, slice(0, 8))
+                st_v2(last, slice(8, 16))
+            if p <= last:
+                st_h2(p)
+            if p < last and GP_J > 0:
+                st_z(p)
+            if p in (3, 5, 7):
+                ch = (p - 3) // 2
+                for q in range(4):
+                    out_bank(ch, q, scopy, "tp")
+                out_store(ch)
+            if p + 2 <= last:
+                w_quant_kv(p + 2)
+            if p <= last:
+                w_quant_q(p)
+                st_v1(p)
+            if p + 3 <= last:
+                w_transpose_kv(p + 3)
+            if p + 1 <= last:
+                w_transpose_q(p + 1)

@@ -154,11 +154,11 @@ def tile_attentionconv_kernel(tc, x, W_qkv, b_qkv, out):
                 )
             scopy(out=dst, in_=wt[:].rearrange("p (g u) o -> p g o u", g=2, u=2))
 
-        def w_transpose_kv(c):
-            wg_kv[c] = work2.tile([P, 2048], BF16, name="wgkv", tag="wgkv", align_bytes=64)
+        def w_transpose_kv(c, t):
+            if t == 0:
+                wg_kv[c] = work2.tile([P, 2048], BF16, name="wgkv", tag="wgkv", align_bytes=64)
             v = wg_kv[c][:].bitcast(F32).rearrange("p (t g o u) -> p t g o u", t=2, g=2, o=P, u=2)
-            w_bank(c, 1, v[:, 0])
-            w_bank(c, 2, v[:, 1])
+            w_bank(c, 1 + t, v[:, t])
 
         def w_transpose_q(c):
             wg_q[c] = work2.tile([P, 1024], BF16, name="wgq", tag="wgq", align_bytes=64)
@@ -228,9 +228,8 @@ def tile_attentionconv_kernel(tc, x, W_qkv, b_qkv, out):
                 bias=bias[:, 8 + c : 9 + c], scale=1.0,
             )
 
-        def mx_q(c):
-            for half in range(2):
-                q_ps[(c, half)] = mx(wc_q[c], ws_q[c], 0, half, "acc2")
+        def mx_q(c, half):
+            q_ps[(c, half)] = mx(wc_q[c], ws_q[c], 0, half, "acc2")
 
         def stt(o, a, s, b, op0, op1):
             nc.vector.scalar_tensor_tensor(out=o, in0=a, scalar=s, in1=b, op0=op0, op1=op1)
@@ -314,7 +313,8 @@ def tile_attentionconv_kernel(tc, x, W_qkv, b_qkv, out):
         x_bank(1, "acc0", scopy)
         x_bank(2, "acc1", vcopy)
         x_bank(3, "acc1", scopy)
-        w_transpose_kv(0)
+        w_transpose_kv(0, 0)
+        w_transpose_kv(0, 1)
         x_bank(4, "acc2", vcopy)
         x_bank(5, "acc2", scopy)
         w_quant_kv(0)
@@ -322,13 +322,15 @@ def tile_attentionconv_kernel(tc, x, W_qkv, b_qkv, out):
         x_quant(0, 1)
         x_bank(6, "acc0", scopy)
         x_bank(7, "acc1", scopy)
-        w_transpose_kv(1)
+        w_transpose_kv(1, 0)
+        w_transpose_kv(1, 1)
         front(0, 0)
         x_quant(1, 0)
         x_quant(1, 1)
         front(0, 1)
         w_quant_kv(1)
-        w_transpose_kv(2)
+        w_transpose_kv(2, 0)
+        w_transpose_kv(2, 1)
         w_transpose_q(0)
 
         last = NCHUNK - 1
@@ -352,9 +354,14 @@ def tile_attentionconv_kernel(tc, x, W_qkv, b_qkv, out):
             if p + 1 <= last:
                 borders(p + 1)
                 front(p + 1, 0)
+            if p + 3 <= last:
+                w_transpose_kv(p + 3, 0)
+            if p + 1 <= last:
                 front(p + 1, 1)
+            if p + 3 <= last:
+                w_transpose_kv(p + 3, 1)
             if 1 <= p <= last + 1:
-                mx_q(p - 1)
+                mx_q(p - 1, 0)
             if p <= last:
                 st_h1(p)
             if 1 <= p <= last and GP_J < 16:
@@ -366,17 +373,18 @@ def tile_attentionconv_kernel(tc, x, W_qkv, b_qkv, out):
                 st_h2(p)
             if p < last and GP_J > 0:
                 st_z(p)
-            if p in (3, 5, 7):
-                ch = (p - 3) // 2
-                for q in range(4):
-                    out_bank(ch, q, scopy, "tp")
-                out_store(ch)
+            if p + 1 <= last:
+                w_transpose_q(p + 1)
+            if 1 <= p <= last + 1:
+                mx_q(p - 1, 1)
+            if 3 <= p <= last + 1:
+                ch, second = divmod(p - 3, 2)
+                out_bank(ch, 2 * second, scopy, "tp")
+                out_bank(ch, 2 * second + 1, scopy, "tp")
+                if second:
+                    out_store(ch)
             if p + 2 <= last:
                 w_quant_kv(p + 2)
             if p <= last:
                 w_quant_q(p)
                 st_v1(p)
-            if p + 3 <= last:
-                w_transpose_kv(p + 3)
-            if p + 1 <= last:
-                w_transpose_q(p + 1)

@@ -44,14 +44,14 @@ def tile_attentionconv_kernel(tc, x, W_qkv, b_qkv, out):
             return pool.tile([P, 4, P], F32, name="bk", tag=tag)
 
         b_rows = const.tile([24, P], BF16, name="b_rows")
-        nc.sync.dma_start(out=b_rows[:], in_=b_qkv.rearrange("(t p) -> t p", p=P))
-        x_rows = x.rearrange("b (g l) (i r) w -> l i (b g) (r w)", l=2, r=16)
+        nc.scalar.dma_start(out=b_rows[:], in_=b_qkv.rearrange("(t p) -> t p", p=P))
+        x_rows = x.rearrange("b (g l) (i a r) w -> l a i (b g) (r w)", l=2, a=2, r=8)
         w_view = W_qkv.rearrange("(s c p) k -> c p s k", s=3, c=NCHUNK, p=P)
         xn = [xpool.tile([P, 4096], BF16, name="xn%d" % h) for h in range(2)]
         wn = [wnat.tile([P, 3, 1024], BF16, name="wn", tag="wn") for c in range(NCHUNK)]
 
-        def load_x(h):
-            nc.sync.dma_start(out=xn[h][:], in_=x_rows[h])
+        def load_x(l, a):
+            nc.sync.dma_start(out=xn[l][:, a * 2048 : (a + 1) * 2048], in_=x_rows[l][a])
 
         def load_kv(c):
             nc.sync.dma_start(out=wn[c][:, 1:3, :], in_=w_view[c][:, 1:3, :])
@@ -59,9 +59,10 @@ def tile_attentionconv_kernel(tc, x, W_qkv, b_qkv, out):
         def load_q(c):
             nc.sync.dma_start(out=wn[c][:, 0:1, :], in_=w_view[c][:, 0:1, :])
 
-        load_x(0)
-        load_x(1)
         load_kv(0)
+        for l in range(2):
+            for a in range(2):
+                load_x(l, a)
         load_kv(1)
         load_q(0)
         for c in range(2, NCHUNK):
@@ -114,11 +115,12 @@ def tile_attentionconv_kernel(tc, x, W_qkv, b_qkv, out):
         xc = [xpool.tile([P, NPATCH], U32, name="xc%d" % g, align_bytes=64) for g in range(2)]
         xs = [xpool.tile([P, NPATCH], U8, name="xs%d" % g, align_bytes=64) for g in range(2)]
 
-        def x_reorder(l, q, copy):
+        def x_reorder(l, a, j0, j1, copy):
             src = xn[l][:].bitcast(F32).rearrange("p (r j s u) -> p u j r s", r=16, j=16, s=4, u=2)
             dst = xr[:].rearrange("p (j u l r s) -> p u l j r s", j=16, u=2, l=2, r=16, s=4)
+            rows = slice(8 * a, 8 * a + 8)
             for u in range(2):
-                copy(out=dst[:, u, l, 4 * q : 4 * q + 4], in_=src[:, u, 4 * q : 4 * q + 4])
+                copy(out=dst[:, u, l, j0:j1, rows], in_=src[:, u, j0:j1, rows])
 
         def x_bank(jp, tag, copy):
             t = bank(tag)
@@ -306,32 +308,30 @@ def tile_attentionconv_kernel(tc, x, W_qkv, b_qkv, out):
                 )
 
         borders(0)
+        w_transpose_kv(0, 0)
+        w_transpose_kv(0, 1)
         for l in range(2):
-            for q in range(4):
-                x_reorder(l, q, scopy if q == 1 else vcopy)
+            for a in range(2):
+                x_reorder(l, a, 0, 10, vcopy)
+                x_reorder(l, a, 10, 16, scopy)
+                if l == 0 and a == 1:
+                    w_quant_kv(0)
         x_bank(0, "acc0", vcopy)
         x_bank(1, "acc0", scopy)
         x_bank(2, "acc1", vcopy)
         x_bank(3, "acc1", scopy)
-        w_transpose_kv(0, 0)
-        w_transpose_kv(0, 1)
-        x_bank(4, "acc2", vcopy)
-        x_bank(5, "acc2", scopy)
-        w_quant_kv(0)
+        x_bank(4, "acc2", scopy)
         x_quant(0, 0)
         x_quant(0, 1)
-        x_bank(6, "acc0", scopy)
-        x_bank(7, "acc1", scopy)
-        w_transpose_kv(1, 0)
-        w_transpose_kv(1, 1)
+        x_bank(5, "acc2", vcopy)
+        x_bank(6, "tp", scopy)
+        x_bank(7, "tp", vcopy)
         front(0, 0)
         x_quant(1, 0)
         x_quant(1, 1)
         front(0, 1)
-        w_quant_kv(1)
-        w_transpose_kv(2, 0)
-        w_transpose_kv(2, 1)
-        w_transpose_q(0)
+        w_transpose_kv(1, 0)
+        w_transpose_kv(1, 1)
 
         last = NCHUNK - 1
         for p in range(NCHUNK + 2):
@@ -351,6 +351,11 @@ def tile_attentionconv_kernel(tc, x, W_qkv, b_qkv, out):
                 out_bank(3, 2, vcopy, "acc0")
                 out_bank(3, 3, scopy, "acc1")
                 out_store(3)
+            if p == 0:
+                w_quant_kv(1)
+                w_transpose_q(0)
+                w_transpose_kv(2, 0)
+                w_transpose_kv(2, 1)
             if p + 1 <= last:
                 borders(p + 1)
                 front(p + 1, 0)

@@ -44,7 +44,7 @@ def tile_attentionconv_kernel(tc, x, W_qkv, b_qkv, out):
             return pool.tile([P, 4, P], F32, name="bk", tag=tag)
 
         b_rows = const.tile([24, P], BF16, name="b_rows")
-        nc.scalar.dma_start(out=b_rows[:], in_=b_qkv.rearrange("(t p) -> t p", p=P))
+        nc.sync.dma_start(out=b_rows[:], in_=b_qkv.rearrange("(t p) -> t p", p=P))
         x_rows = x.rearrange("b (g l) (i a r) w -> l a i (b g) (r w)", l=2, a=2, r=8)
         w_view = W_qkv.rearrange("(s c p) k -> c p s k", s=3, c=NCHUNK, p=P)
         xn = [xpool.tile([P, 4096], BF16, name="xn%d" % h) for h in range(2)]
@@ -74,6 +74,8 @@ def tile_attentionconv_kernel(tc, x, W_qkv, b_qkv, out):
         make_identity(nc, ident[:])
         pidx = const.tile([P, 1], I32, name="pidx")
         nc.gpsimd.iota(pidx[:], pattern=[[0, 1]], base=0, channel_multiplier=1)
+        zeros = const.tile([P, BANK], BF16, name="zeros")
+        nc.gpsimd.memset(zeros[:], 0.0)
         ones = const.tile([P, P], F32, name="ones")
         nc.gpsimd.memset(ones[:], 1.0)
         s_i = const.tile([P, 1], I32, name="s_i")
@@ -231,7 +233,7 @@ def tile_attentionconv_kernel(tc, x, W_qkv, b_qkv, out):
             )
 
         def mx_q(c, half):
-            q_ps[(c, half)] = mx(wc_q[c], ws_q[c], 0, half, "acc2")
+            q_ps[(c, half)] = mx(wc_q[c], ws_q[c], 0, half, "acc2" if c < NCHUNK - 1 else "acc1")
 
         def stt(o, a, s, b, op0, op1):
             nc.vector.scalar_tensor_tensor(out=o, in0=a, scalar=s, in1=b, op0=op0, op1=op1)
@@ -260,15 +262,22 @@ def tile_attentionconv_kernel(tc, x, W_qkv, b_qkv, out):
             ut[c] = work2.tile([P, 16, YJ], F32, name="ut", tag="ut")
             stt(qt[c][:], tt[c][:, :, 4:68], tab[:, 2 + rh : 3 + rh], tt[c][:, :, 8:72], ALU.mult, ALU.add)
 
+        def gp_rows(c):
+            return GP_J if c < NCHUNK - 1 else 8
+
         def st_z(c):
             rh = c % 2
+            nj = gp_rows(c)
             zt[c] = work2.tile([P, GP_J, YJ], F32, name="zt", tag="zt")
             nc.scalar.activation(
-                out=zt[c][:], in_=tt[c][:, 0:GP_J, 12:76], func=ACT.Copy, scale=tab[:, 4 + rh : 5 + rh]
+                out=zt[c][:, 0:nj, :], in_=tt[c][:, 0:nj, 12:76], func=ACT.Copy, scale=tab[:, 4 + rh : 5 + rh]
             )
 
         def st_g(c):
-            nc.gpsimd.tensor_tensor(out=ut[c][:, 0:GP_J, :], in0=qt[c][:, 0:GP_J, :], in1=zt[c][:], op=ALU.add)
+            nj = gp_rows(c)
+            nc.gpsimd.tensor_tensor(
+                out=ut[c][:, 0:nj, :], in0=qt[c][:, 0:nj, :], in1=zt[c][:, 0:nj, :], op=ALU.add
+            )
 
         def st_v2(c, js):
             rh = c % 2
@@ -307,9 +316,22 @@ def tile_attentionconv_kernel(tc, x, W_qkv, b_qkv, out):
                     out=out[b, ch].rearrange("(m r) w -> m (r w)", r=8), in_=os_flat[b : b + 125 : 4, :]
                 )
 
+        def out_store_half(ch, half):
+            px = slice(half * 128, (half + 1) * 128)
+            for b in range(4):
+                nc.sync.dma_start(
+                    out=out[b, ch].rearrange("(m r) w -> m r w", r=8)[:, :, px],
+                    in_=os_tiles[ch][b : b + 125 : 4, :, 8 * half : 8 * half + 8, :],
+                )
+
         borders(0)
         w_transpose_kv(0, 0)
         w_transpose_kv(0, 1)
+        warm = bank("acc2")
+        for d in range(4):
+            nc.tensor.matmul(
+                out=warm[:].rearrange("p a b -> p (a b)"), lhsT=zeros[:, 0:P], rhs=zeros[:], start=True, stop=True
+            )
         for l in range(2):
             for a in range(2):
                 x_reorder(l, a, 0, 10, vcopy)
@@ -329,67 +351,71 @@ def tile_attentionconv_kernel(tc, x, W_qkv, b_qkv, out):
         front(0, 0)
         x_quant(1, 0)
         x_quant(1, 1)
-        front(0, 1)
         w_transpose_kv(1, 0)
         w_transpose_kv(1, 1)
+        front(0, 1)
 
         last = NCHUNK - 1
-        for p in range(NCHUNK + 2):
-            if p <= last:
-                st_k(p, 0)
-                st_k(p, 1)
-            if 1 <= p <= last and GP_J > 0:
-                st_g(p - 1)
-            if 2 <= p <= last + 1:
-                st_f(p - 2, 0)
-                st_f(p - 2, 1)
-            if p == last + 2:
-                st_f(last, 0)
-                out_bank(3, 0, scopy, "tp")
-                out_bank(3, 1, scopy, "tp")
-                st_f(last, 1)
-                out_bank(3, 2, vcopy, "acc0")
-                out_bank(3, 3, scopy, "acc1")
-                out_store(3)
+        for p in range(NCHUNK):
+            st_k(p, 0)
             if p == 0:
                 w_quant_kv(1)
-                w_transpose_q(0)
-                w_transpose_kv(2, 0)
-                w_transpose_kv(2, 1)
+            st_k(p, 1)
+            if p >= 1:
+                st_g(p - 1)
+            if p >= 2:
+                st_f(p - 2, 0)
+                st_f(p - 2, 1)
+            if p == 0:
+                st_h1(0)
             if p + 1 <= last:
                 borders(p + 1)
                 front(p + 1, 0)
-            if p + 3 <= last:
-                w_transpose_kv(p + 3, 0)
+            if p + 2 <= last:
+                w_transpose_kv(p + 2, 0)
             if p + 1 <= last:
                 front(p + 1, 1)
-            if p + 3 <= last:
-                w_transpose_kv(p + 3, 1)
-            if 1 <= p <= last + 1:
+            if p + 2 <= last:
+                w_transpose_kv(p + 2, 1)
+            if p == 0:
+                w_transpose_q(0)
+            if p >= 1:
                 mx_q(p - 1, 0)
-            if p <= last:
                 st_h1(p)
-            if 1 <= p <= last and GP_J < 16:
+                w_quant_q(p)
+            st_h2(p)
+            if p >= 1:
                 st_v2(p - 1, slice(GP_J, 16))
-            if p == last + 1:
-                st_v2(last, slice(0, 8))
-                st_v2(last, slice(8, 16))
-            if p <= last:
-                st_h2(p)
-            if p < last and GP_J > 0:
-                st_z(p)
+            st_z(p)
             if p + 1 <= last:
                 w_transpose_q(p + 1)
-            if 1 <= p <= last + 1:
+            if p >= 1:
                 mx_q(p - 1, 1)
-            if 3 <= p <= last + 1:
+            if p >= 3:
                 ch, second = divmod(p - 3, 2)
                 out_bank(ch, 2 * second, scopy, "tp")
                 out_bank(ch, 2 * second + 1, scopy, "tp")
-                if second:
+                if p == last:
+                    mx_q(last, 0)
+                    mx_q(last, 1)
+                    out_bank(ch, 2, scopy, "tp")
+                    out_bank(ch, 3, scopy, "tp")
+                if second or p == last:
                     out_store(ch)
+            st_v1(p)
             if p + 2 <= last:
                 w_quant_kv(p + 2)
-            if p <= last:
-                w_quant_q(p)
-                st_v1(p)
+            if p == 0:
+                w_quant_q(0)
+        st_g(last)
+        st_f(last - 1, 0)
+        st_f(last - 1, 1)
+        st_v2(last, slice(8, 16))
+        st_f(last, 0)
+        out_bank(3, 0, scopy, "tp")
+        out_bank(3, 1, scopy, "tp")
+        out_store_half(3, 0)
+        st_f(last, 1)
+        out_bank(3, 2, vcopy, "acc0")
+        out_bank(3, 3, scopy, "acc0")
+        out_store_half(3, 1)

@@ -74,8 +74,6 @@ def tile_attentionconv_kernel(tc, x, W_qkv, b_qkv, out):
         make_identity(nc, ident[:])
         pidx = const.tile([P, 1], I32, name="pidx")
         nc.gpsimd.iota(pidx[:], pattern=[[0, 1]], base=0, channel_multiplier=1)
-        zeros = const.tile([P, BANK], BF16, name="zeros")
-        nc.gpsimd.memset(zeros[:], 0.0)
         ones = const.tile([P, P], F32, name="ones")
         nc.gpsimd.memset(ones[:], 1.0)
         s_i = const.tile([P, 1], I32, name="s_i")
@@ -327,11 +325,6 @@ def tile_attentionconv_kernel(tc, x, W_qkv, b_qkv, out):
         borders(0)
         w_transpose_kv(0, 0)
         w_transpose_kv(0, 1)
-        warm = bank("acc2")
-        for d in range(4):
-            nc.tensor.matmul(
-                out=warm[:].rearrange("p a b -> p (a b)"), lhsT=zeros[:, 0:P], rhs=zeros[:], start=True, stop=True
-            )
         for l in range(2):
             for a in range(2):
                 x_reorder(l, a, 0, 10, vcopy)

@@ -45,13 +45,13 @@ def tile_attentionconv_kernel(tc, x, W_qkv, b_qkv, out):
 
         b_rows = const.tile([24, P], BF16, name="b_rows")
         nc.sync.dma_start(out=b_rows[:], in_=b_qkv.rearrange("(t p) -> t p", p=P))
-        x_rows = x.rearrange("b (g l) (i a r) w -> l a i (b g) (r w)", l=2, a=2, r=8)
+        x_rows = x.rearrange("b (g l) (i r) w -> l (b g) i (r w)", l=2, r=16)
         w_view = W_qkv.rearrange("(s c p) k -> c p s k", s=3, c=NCHUNK, p=P)
         xn = [xpool.tile([P, 4096], BF16, name="xn%d" % h) for h in range(2)]
         wn = [wnat.tile([P, 3, 1024], BF16, name="wn", tag="wn") for c in range(NCHUNK)]
 
-        def load_x(l, a):
-            nc.sync.dma_start(out=xn[l][:, a * 2048 : (a + 1) * 2048], in_=x_rows[l][a])
+        def load_x(l, q, queue):
+            queue.dma_start(out=xn[l][q : q + 121 : 8, :], in_=x_rows[l][q])
 
         def load_kv(c):
             nc.sync.dma_start(out=wn[c][:, 1:3, :], in_=w_view[c][:, 1:3, :])
@@ -61,8 +61,9 @@ def tile_attentionconv_kernel(tc, x, W_qkv, b_qkv, out):
 
         load_kv(0)
         for l in range(2):
-            for a in range(2):
-                load_x(l, a)
+            for q in range(4):
+                load_x(l, q, nc.sync)
+                load_x(l, q + 4, nc.scalar)
         load_kv(1)
         load_q(0)
         for c in range(2, NCHUNK):

@@ -44,7 +44,6 @@ def tile_attentionconv_kernel(tc, x, W_qkv, b_qkv, out):
             return pool.tile([P, 4, P], F32, name="bk", tag=tag)
 
         b_rows = const.tile([24, P], BF16, name="b_rows")
-        nc.sync.dma_start(out=b_rows[:], in_=b_qkv.rearrange("(t p) -> t p", p=P))
         x_rows = x.rearrange("b (g l) (i r) w -> l (b g) i (r w)", l=2, r=16)
         w_view = W_qkv.rearrange("(s c p) k -> c p s k", s=3, c=NCHUNK, p=P)
         xn = [xpool.tile([P, 4096], BF16, name="xn%d" % h) for h in range(2)]
@@ -59,17 +58,13 @@ def tile_attentionconv_kernel(tc, x, W_qkv, b_qkv, out):
         def load_q(c):
             nc.sync.dma_start(out=wn[c][:, 0:1, :], in_=w_view[c][:, 0:1, :])
 
+        for q in range(4, 8):
+            load_x(0, q, nc.scalar)
+        nc.sync.dma_start(out=b_rows[:], in_=b_qkv.rearrange("(t p) -> t p", p=P))
         load_kv(0)
         for l in range(2):
             for q in range(4):
                 load_x(l, q, nc.sync)
-                load_x(l, q + 4, nc.scalar)
-        load_kv(1)
-        load_q(0)
-        for c in range(2, NCHUNK):
-            load_kv(c)
-            load_q(c - 1)
-        load_q(NCHUNK - 1)
 
         ident = const.tile([P, P], F32, name="ident")
         make_identity(nc, ident[:])
@@ -95,12 +90,16 @@ def tile_attentionconv_kernel(tc, x, W_qkv, b_qkv, out):
             nc.scalar.activation(
                 out=tab[:, 4 + rh : 5 + rh], in_=r_f[:], func=ACT.Exp, scale=-0.125, bias=-1.0 * rh
             )
+        for q in range(4, 8):
+            load_x(1, q, nc.scalar)
+        load_kv(1)
+        load_q(0)
+        for c in range(2, NCHUNK):
+            load_kv(c)
+            load_q(c - 1)
+        load_q(NCHUNK - 1)
         b_rows_f = const.tile([P, P], F32, name="b_rows_f")
         nc.vector.memset(b_rows_f[:], 0.0)
-        hs = const.tile([P, 1], F32, name="hs")
-        nc.vector.scalar_tensor_tensor(
-            out=hs[:], in0=tab[:, 0:1], scalar=1.0, in1=tab[:, 1:2], op0=ALU.add, op1=ALU.add
-        )
         vcopy(out=b_rows_f[0:24, :], in_=b_rows[:])
         b_ps = bank("tp")
         nc.tensor.transpose(out=b_ps[:, 0, :], in_=b_rows_f[:], identity=ident[:])
@@ -108,6 +107,10 @@ def tile_attentionconv_kernel(tc, x, W_qkv, b_qkv, out):
         vcopy(out=bias[:], in_=b_ps[:, 0, 0:24])
         cb = const.tile([P, NCHUNK], F32, name="cb")
         nc.vector.tensor_mul(out=cb[:], in0=bias[:, 8:16], in1=bias[:, 16:24])
+        hs = const.tile([P, 1], F32, name="hs")
+        nc.vector.scalar_tensor_tensor(
+            out=hs[:], in0=tab[:, 0:1], scalar=1.0, in1=tab[:, 1:2], op0=ALU.add, op1=ALU.add
+        )
         cbh = const.tile([P, NCHUNK], F32, name="cbh")
         nc.vector.tensor_scalar_mul(out=cbh[:], in0=cb[:], scalar1=hs[:, 0:1])
 
@@ -117,11 +120,10 @@ def tile_attentionconv_kernel(tc, x, W_qkv, b_qkv, out):
         xs = [xpool.tile([P, NPATCH], U8, name="xs%d" % g, align_bytes=64) for g in range(2)]
 
         def x_reorder(l, a, j0, j1, copy):
-            src = xn[l][:].bitcast(F32).rearrange("p (r j s u) -> p u j r s", r=16, j=16, s=4, u=2)
-            dst = xr[:].rearrange("p (j u l r s) -> p u l j r s", j=16, u=2, l=2, r=16, s=4)
+            src = xn[l][:].bitcast(F32).rearrange("p (r j s u) -> p j r s u", r=16, j=16, s=4, u=2)
+            dst = xr[:].rearrange("p (j u l r s) -> p l j r s u", j=16, u=2, l=2, r=16, s=4)
             rows = slice(8 * a, 8 * a + 8)
-            for u in range(2):
-                copy(out=dst[:, u, l, j0:j1, rows], in_=src[:, u, j0:j1, rows])
+            copy(out=dst[:, l, j0:j1, rows], in_=src[:, j0:j1, rows])
 
         def x_bank(jp, tag, copy):
             t = bank(tag)

@@ -44,13 +44,13 @@ def tile_attentionconv_kernel(tc, x, W_qkv, b_qkv, out):
             return pool.tile([P, 4, P], F32, name="bk", tag=tag)
 
         b_rows = const.tile([24, P], BF16, name="b_rows")
-        x_rows = x.rearrange("b (g l) (i r) w -> l (b g) i (r w)", l=2, r=16)
+        x_rows = x.rearrange("(z b) (g l) (i r) w -> l (b g) i z (r w)", z=2, l=2, r=16)
         w_view = W_qkv.rearrange("(s c p) k -> c p s k", s=3, c=NCHUNK, p=P)
         xn = [xpool.tile([P, 4096], BF16, name="xn%d" % h) for h in range(2)]
         wn = [wnat.tile([P, 3, 1024], BF16, name="wn", tag="wn") for c in range(NCHUNK)]
 
-        def load_x(l, q, queue):
-            queue.dma_start(out=xn[l][q : q + 121 : 8, :], in_=x_rows[l][q])
+        def load_x(l, q):
+            nc.sync.dma_start(out=xn[l][q : q + 125 : 4, :], in_=x_rows[l][q])
 
         def load_kv(c):
             nc.sync.dma_start(out=wn[c][:, 1:3, :], in_=w_view[c][:, 1:3, :])
@@ -58,13 +58,17 @@ def tile_attentionconv_kernel(tc, x, W_qkv, b_qkv, out):
         def load_q(c):
             nc.sync.dma_start(out=wn[c][:, 0:1, :], in_=w_view[c][:, 0:1, :])
 
-        for q in range(4, 8):
-            load_x(0, q, nc.scalar)
         nc.sync.dma_start(out=b_rows[:], in_=b_qkv.rearrange("(t p) -> t p", p=P))
         load_kv(0)
         for l in range(2):
             for q in range(4):
-                load_x(l, q, nc.sync)
+                load_x(l, q)
+        load_kv(1)
+        load_q(0)
+        for c in range(2, NCHUNK):
+            load_kv(c)
+            load_q(c - 1)
+        load_q(NCHUNK - 1)
 
         ident = const.tile([P, P], F32, name="ident")
         make_identity(nc, ident[:])
@@ -90,14 +94,6 @@ def tile_attentionconv_kernel(tc, x, W_qkv, b_qkv, out):
             nc.scalar.activation(
                 out=tab[:, 4 + rh : 5 + rh], in_=r_f[:], func=ACT.Exp, scale=-0.125, bias=-1.0 * rh
             )
-        for q in range(4, 8):
-            load_x(1, q, nc.scalar)
-        load_kv(1)
-        load_q(0)
-        for c in range(2, NCHUNK):
-            load_kv(c)
-            load_q(c - 1)
-        load_q(NCHUNK - 1)
         b_rows_f = const.tile([P, P], F32, name="b_rows_f")
         nc.vector.memset(b_rows_f[:], 0.0)
         vcopy(out=b_rows_f[0:24, :], in_=b_rows[:])

@@ -20,7 +20,8 @@ NPATCH = 1024
 BANK = 512
 YJ = 64
 TROW = 80
-GP_J = 12
+WARM = 6
+GP_J = 10
 
 
 def tile_attentionconv_kernel(tc, x, W_qkv, b_qkv, out):
@@ -115,11 +116,10 @@ def tile_attentionconv_kernel(tc, x, W_qkv, b_qkv, out):
         xc = [xpool.tile([P, NPATCH], U32, name="xc%d" % g, align_bytes=64) for g in range(2)]
         xs = [xpool.tile([P, NPATCH], U8, name="xs%d" % g, align_bytes=64) for g in range(2)]
 
-        def x_reorder(l, a, j0, j1, copy):
+        def x_reorder(l, j0, j1, copy):
             src = xn[l][:].bitcast(F32).rearrange("p (r j s u) -> p j r s u", r=16, j=16, s=4, u=2)
             dst = xr[:].rearrange("p (j u l r s) -> p l j r s u", j=16, u=2, l=2, r=16, s=4)
-            rows = slice(8 * a, 8 * a + 8)
-            copy(out=dst[:, l, j0:j1, rows], in_=src[:, j0:j1, rows])
+            copy(out=dst[:, l, j0:j1], in_=src[:, j0:j1])
 
         def x_bank(jp, tag, copy):
             t = bank(tag)
@@ -260,7 +260,7 @@ def tile_attentionconv_kernel(tc, x, W_qkv, b_qkv, out):
             stt(qt[c][:], tt[c][:, :, 4:68], tab[:, 2 + rh : 3 + rh], tt[c][:, :, 8:72], ALU.mult, ALU.add)
 
         def gp_rows(c):
-            return GP_J if c < NCHUNK - 1 else 8
+            return 6 if c == 0 else 8 if c == NCHUNK - 1 else GP_J
 
         def st_z(c):
             rh = c % 2
@@ -321,15 +321,21 @@ def tile_attentionconv_kernel(tc, x, W_qkv, b_qkv, out):
                     in_=os_tiles[ch][b : b + 125 : 4, :, 8 * half : 8 * half + 8, :],
                 )
 
+        def warm_up(n):
+            t = bank("acc2")
+            data = xr[:].bitcast(BF16).rearrange("p (m l w) -> p l m w", m=32, l=2, w=P)[:, 0]
+            for i in range(n):
+                nc.tensor.matmul(out=t[:], lhsT=data[:, 0, :], rhs=data[:, 0:4, :], start=True, stop=True)
+
         borders(0)
         w_transpose_kv(0, 0)
         w_transpose_kv(0, 1)
         for l in range(2):
-            for a in range(2):
-                x_reorder(l, a, 0, 10, vcopy)
-                x_reorder(l, a, 10, 16, scopy)
-                if l == 0 and a == 1:
-                    w_quant_kv(0)
+            x_reorder(l, 0, 10, vcopy)
+            x_reorder(l, 10, 16, scopy)
+            if l == 0:
+                w_quant_kv(0)
+                warm_up(WARM)
         x_bank(0, "acc0", vcopy)
         x_bank(1, "acc0", scopy)
         x_bank(2, "acc1", vcopy)
@@ -337,15 +343,16 @@ def tile_attentionconv_kernel(tc, x, W_qkv, b_qkv, out):
         x_bank(4, "acc2", scopy)
         x_quant(0, 0)
         x_quant(0, 1)
-        x_bank(5, "acc2", vcopy)
-        x_bank(6, "tp", scopy)
-        x_bank(7, "tp", vcopy)
+        x_bank(5, "acc2", scopy)
+        x_bank(6, "tp", vcopy)
+        x_bank(7, "tp", scopy)
         front(0, 0)
         x_quant(1, 0)
         x_quant(1, 1)
         w_transpose_kv(1, 0)
         w_transpose_kv(1, 1)
         front(0, 1)
+        w_transpose_kv(2, 0)
 
         last = NCHUNK - 1
         for p in range(NCHUNK):
@@ -364,20 +371,20 @@ def tile_attentionconv_kernel(tc, x, W_qkv, b_qkv, out):
                 borders(p + 1)
                 front(p + 1, 0)
             if p + 2 <= last:
-                w_transpose_kv(p + 2, 0)
+                w_transpose_kv(p + 2, 1 if p == 0 else 0)
             if p + 1 <= last:
                 front(p + 1, 1)
-            if p + 2 <= last:
-                w_transpose_kv(p + 2, 1)
             if p == 0:
                 w_transpose_q(0)
+            elif p + 2 <= last:
+                w_transpose_kv(p + 2, 1)
             if p >= 1:
                 mx_q(p - 1, 0)
                 st_h1(p)
                 w_quant_q(p)
             st_h2(p)
             if p >= 1:
-                st_v2(p - 1, slice(GP_J, 16))
+                st_v2(p - 1, slice(gp_rows(p - 1), 16))
             st_z(p)
             if p + 1 <= last:
                 w_transpose_q(p + 1)

@@ -21,7 +21,7 @@ BANK = 512
 YJ = 64
 TROW = 80
 WARM = 6
-GP_J = 10
+GP_J = 12
 
 
 def tile_attentionconv_kernel(tc, x, W_qkv, b_qkv, out):
@@ -33,16 +33,18 @@ def tile_attentionconv_kernel(tc, x, W_qkv, b_qkv, out):
         work3 = ctx.enter_context(tc.tile_pool(name="work3", bufs=3))
         work2 = ctx.enter_context(tc.tile_pool(name="work2", bufs=2))
         work1 = ctx.enter_context(tc.tile_pool(name="work1", bufs=1))
-        ps_mx = ctx.enter_context(tc.psum_pool(name="ps_mx", bufs=2))
-        ps_tp = ctx.enter_context(tc.psum_pool(name="ps_tp", bufs=2))
+        ps_k = ctx.enter_context(tc.psum_pool(name="ps_k", bufs=1))
+        ps_vq = ctx.enter_context(tc.psum_pool(name="ps_vq", bufs=2))
+        ps_tp = ctx.enter_context(tc.psum_pool(name="ps_tp", bufs=3))
         ctx.enter_context(tc.manual_schedule())
 
         vcopy = nc.vector.tensor_copy
         scopy = nc.scalar.copy
 
+        banks = {"k": ps_k, "v": ps_vq, "q": ps_vq, "tp": ps_tp}
+
         def bank(tag):
-            pool = ps_tp if tag == "tp" else ps_mx
-            return pool.tile([P, 4, P], F32, name="bk", tag=tag)
+            return banks[tag].tile([P, 4, P], F32, name="bk", tag=tag)
 
         b_rows = const.tile([24, P], BF16, name="b_rows")
         x_rows = x.rearrange("(z b) (g l) (i r) w -> l (b g) i z (r w)", z=2, l=2, r=16)
@@ -112,9 +114,9 @@ def tile_attentionconv_kernel(tc, x, W_qkv, b_qkv, out):
         nc.vector.tensor_scalar_mul(out=cbh[:], in0=cb[:], scalar1=hs[:, 0:1])
 
         xr = xpool.tile([P, 4096], F32, name="xr")
-        xg = [xpool.tile([P, 4096], BF16, name="xg%d" % g, align_bytes=64) for g in range(2)]
-        xc = [xpool.tile([P, NPATCH], U32, name="xc%d" % g, align_bytes=64) for g in range(2)]
-        xs = [xpool.tile([P, NPATCH], U8, name="xs%d" % g, align_bytes=64) for g in range(2)]
+        xg = xpool.tile([P, 8192], BF16, name="xg", align_bytes=64)
+        xc = xpool.tile([P, 2048], U32, name="xc", align_bytes=64)
+        xs = xpool.tile([P, 2048], U8, name="xs", align_bytes=64)
 
         def x_reorder(l, j0, j1, copy):
             src = xn[l][:].bitcast(F32).rearrange("p (r j s u) -> p j r s u", r=16, j=16, s=4, u=2)
@@ -127,15 +129,15 @@ def tile_attentionconv_kernel(tc, x, W_qkv, b_qkv, out):
                 c0 = (4 * jp + ju) * P
                 nc.tensor.transpose(out=t[:, ju, :], in_=xr[:, c0 : c0 + P], identity=ident[:])
             src = t[:].rearrange("p (j u) (n g) -> p g j n u", j=2, u=2, n=YJ, g=2)
-            for g in range(2):
-                dst = xg[g][:].bitcast(F32).rearrange("p (j n u) -> p j n u", j=16, n=YJ, u=2)
-                copy(out=dst[:, 2 * jp : 2 * jp + 2], in_=src[:, g])
+            dst = xg[:].bitcast(F32).rearrange("p (h g q j n u) -> p h q g j n u", h=2, g=2, q=4, j=2, n=YJ, u=2)
+            copy(out=dst[:, jp // 4, jp % 4], in_=src)
 
         def x_quant(half, g):
+            b = 2 * half + g
             nc.vector.quantize_mx(
-                out=xc[g][:, half * BANK : (half + 1) * BANK].bitcast(FP8X4),
-                scales=xs[g][:, half * BANK : (half + 1) * BANK],
-                in_=xg[g][:, half * 4 * BANK : (half + 1) * 4 * BANK],
+                out=xc[:, b * BANK : (b + 1) * BANK].bitcast(FP8X4),
+                scales=xs[:, b * BANK : (b + 1) * BANK],
+                in_=xg[:, 4 * b * BANK : 4 * (b + 1) * BANK],
             )
 
         wg_kv = {}
@@ -176,16 +178,16 @@ def tile_attentionconv_kernel(tc, x, W_qkv, b_qkv, out):
             nc.vector.quantize_mx(out=wc_q[c][:].bitcast(FP8X4), scales=ws_q[c][:], in_=wg_q[c][:])
 
         def mx(codes, scales, first, half, tag):
-            acc = ps_mx.tile([P, BANK], F32, name="acc", tag=tag)
-            pats = slice(half * BANK, (half + 1) * BANK)
+            acc = banks[tag].tile([P, BANK], F32, name="acc", tag=tag)
             for g in range(2):
+                pats = slice((2 * half + g) * BANK, (2 * half + g + 1) * BANK)
                 cols = slice(first + g * P, first + (g + 1) * P)
                 nc.tensor.matmul_mx(
                     out=acc[:],
                     lhsT=codes[:, cols].bitcast(FP8X4),
                     lhsT_scale=scales[:, cols],
-                    rhs=xc[g][:, pats].bitcast(FP8X4),
-                    rhs_scale=xs[g][:, pats],
+                    rhs=xc[:, pats].bitcast(FP8X4),
+                    rhs_scale=xs[:, pats],
                     start=(g == 0),
                     stop=(g == 1),
                 )
@@ -222,15 +224,18 @@ def tile_attentionconv_kernel(tc, x, W_qkv, b_qkv, out):
         def front(c, half):
             if half == 0:
                 ks[c] = work2.tile([P, NPATCH], F32, name="ks", tag="ks")
-            k_ps = mx(wc_kv[c], ws_kv[c], 0, half, "acc0")
-            v_ps[(c, half)] = mx(wc_kv[c], ws_kv[c], 256, half, "acc1")
+            if half == 1:
+                v_ps[(c, half)] = mx(wc_kv[c], ws_kv[c], 256, half, "v")
+            k_ps = mx(wc_kv[c], ws_kv[c], 0, half, "k")
+            if half == 0:
+                v_ps[(c, half)] = mx(wc_kv[c], ws_kv[c], 256, half, "v")
             nc.scalar.activation(
                 out=ks[c][:, half * BANK : (half + 1) * BANK], in_=k_ps[:], func=ACT.Identity,
                 bias=bias[:, 8 + c : 9 + c], scale=1.0,
             )
 
         def mx_q(c, half):
-            q_ps[(c, half)] = mx(wc_q[c], ws_q[c], 0, half, "acc2" if c < NCHUNK - 1 else "acc1")
+            q_ps[(c, half)] = mx(wc_q[c], ws_q[c], 0, half, "q" if c < NCHUNK - 1 else "v")
 
         def stt(o, a, s, b, op0, op1):
             nc.vector.scalar_tensor_tensor(out=o, in0=a, scalar=s, in1=b, op0=op0, op1=op1)
@@ -322,7 +327,7 @@ def tile_attentionconv_kernel(tc, x, W_qkv, b_qkv, out):
                 )
 
         def warm_up(n):
-            t = bank("acc2")
+            t = bank("q")
             data = xr[:].bitcast(BF16).rearrange("p (m l w) -> p l m w", m=32, l=2, w=P)[:, 0]
             for i in range(n):
                 nc.tensor.matmul(out=t[:], lhsT=data[:, 0, :], rhs=data[:, 0:4, :], start=True, stop=True)
@@ -336,14 +341,14 @@ def tile_attentionconv_kernel(tc, x, W_qkv, b_qkv, out):
             if l == 0:
                 w_quant_kv(0)
                 warm_up(WARM)
-        x_bank(0, "acc0", vcopy)
-        x_bank(1, "acc0", scopy)
-        x_bank(2, "acc1", vcopy)
-        x_bank(3, "acc1", scopy)
-        x_bank(4, "acc2", scopy)
+        x_bank(0, "v", vcopy)
+        x_bank(1, "v", scopy)
+        x_bank(2, "q", vcopy)
+        x_bank(3, "q", scopy)
+        x_bank(4, "k", scopy)
         x_quant(0, 0)
         x_quant(0, 1)
-        x_bank(5, "acc2", scopy)
+        x_bank(5, "tp", scopy)
         x_bank(6, "tp", vcopy)
         x_bank(7, "tp", scopy)
         front(0, 0)
@@ -360,6 +365,8 @@ def tile_attentionconv_kernel(tc, x, W_qkv, b_qkv, out):
             if p == 0:
                 w_quant_kv(1)
             st_k(p, 1)
+            if p == 1:
+                w_quant_q(0)
             if p >= 1:
                 st_g(p - 1)
             if p >= 2:
@@ -370,16 +377,16 @@ def tile_attentionconv_kernel(tc, x, W_qkv, b_qkv, out):
             if p + 1 <= last:
                 borders(p + 1)
                 front(p + 1, 0)
-            if p + 2 <= last:
-                w_transpose_kv(p + 2, 1 if p == 0 else 0)
-            if p + 1 <= last:
                 front(p + 1, 1)
             if p == 0:
+                w_transpose_kv(2, 1)
                 w_transpose_q(0)
             elif p + 2 <= last:
+                w_transpose_kv(p + 2, 0)
                 w_transpose_kv(p + 2, 1)
             if p >= 1:
                 mx_q(p - 1, 0)
+                mx_q(p - 1, 1)
                 st_h1(p)
                 w_quant_q(p)
             st_h2(p)
@@ -388,8 +395,6 @@ def tile_attentionconv_kernel(tc, x, W_qkv, b_qkv, out):
             st_z(p)
             if p + 1 <= last:
                 w_transpose_q(p + 1)
-            if p >= 1:
-                mx_q(p - 1, 1)
             if p >= 3:
                 ch, second = divmod(p - 3, 2)
                 out_bank(ch, 2 * second, scopy, "tp")
@@ -404,8 +409,6 @@ def tile_attentionconv_kernel(tc, x, W_qkv, b_qkv, out):
             st_v1(p)
             if p + 2 <= last:
                 w_quant_kv(p + 2)
-            if p == 0:
-                w_quant_q(0)
         st_g(last)
         st_f(last - 1, 0)
         st_f(last - 1, 1)
@@ -415,6 +418,6 @@ def tile_attentionconv_kernel(tc, x, W_qkv, b_qkv, out):
         out_bank(3, 1, scopy, "tp")
         out_store_half(3, 0)
         st_f(last, 1)
-        out_bank(3, 2, vcopy, "acc0")
-        out_bank(3, 3, scopy, "acc0")
+        out_bank(3, 2, vcopy, "q")
+        out_bank(3, 3, scopy, "q")
         out_store_half(3, 1)

@@ -20,7 +20,7 @@ NPATCH = 1024
 BANK = 512
 YJ = 64
 TROW = 80
-WARM = 6
+WARM = 3
 GP_J = 12
 
 
@@ -52,8 +52,8 @@ def tile_attentionconv_kernel(tc, x, W_qkv, b_qkv, out):
         xn = [xpool.tile([P, 4096], BF16, name="xn%d" % h) for h in range(2)]
         wn = [wnat.tile([P, 3, 1024], BF16, name="wn", tag="wn") for c in range(NCHUNK)]
 
-        def load_x(l, q):
-            nc.sync.dma_start(out=xn[l][q : q + 125 : 4, :], in_=x_rows[l][q])
+        def load_x(l, q, queue):
+            queue.dma_start(out=xn[l][q : q + 125 : 4, :], in_=x_rows[l][q])
 
         def load_kv(c):
             nc.sync.dma_start(out=wn[c][:, 1:3, :], in_=w_view[c][:, 1:3, :])
@@ -61,11 +61,14 @@ def tile_attentionconv_kernel(tc, x, W_qkv, b_qkv, out):
         def load_q(c):
             nc.sync.dma_start(out=wn[c][:, 0:1, :], in_=w_view[c][:, 0:1, :])
 
+        for l in range(2):
+            for q in (2, 3):
+                load_x(l, q, nc.scalar)
         nc.sync.dma_start(out=b_rows[:], in_=b_qkv.rearrange("(t p) -> t p", p=P))
         load_kv(0)
         for l in range(2):
-            for q in range(4):
-                load_x(l, q)
+            for q in (0, 1):
+                load_x(l, q, nc.sync)
         load_kv(1)
         load_q(0)
         for c in range(2, NCHUNK):

from contextlib import ExitStack

import concourse.mybir as mybir
from concourse.masks import make_identity

F32 = mybir.dt.float32
BF16 = mybir.dt.bfloat16
U32 = mybir.dt.uint32
U8 = mybir.dt.uint8
I32 = mybir.dt.int32
FP8X4 = mybir.dt.float8_e4m3fn_x4
ALU = mybir.AluOpType
ACT = mybir.ActivationFunctionType

FLOPS = 2 * 1024 * 1024 * 3072

P = 128
NCHUNK = 8
NPATCH = 1024
BANK = 512
YJ = 64
TROW = 80
WARM = 3
GP_J = 12


def tile_attentionconv_kernel(tc, x, W_qkv, b_qkv, out):
    nc = tc.nc
    with ExitStack() as ctx:
        const = ctx.enter_context(tc.tile_pool(name="const", bufs=1))
        xpool = ctx.enter_context(tc.tile_pool(name="xpool", bufs=1))
        wnat = ctx.enter_context(tc.tile_pool(name="wnat", bufs=NCHUNK))
        work3 = ctx.enter_context(tc.tile_pool(name="work3", bufs=3))
        work2 = ctx.enter_context(tc.tile_pool(name="work2", bufs=2))
        work1 = ctx.enter_context(tc.tile_pool(name="work1", bufs=1))
        ps_k = ctx.enter_context(tc.psum_pool(name="ps_k", bufs=1))
        ps_vq = ctx.enter_context(tc.psum_pool(name="ps_vq", bufs=2))
        ps_tp = ctx.enter_context(tc.psum_pool(name="ps_tp", bufs=3))
        ctx.enter_context(tc.manual_schedule())

        vcopy = nc.vector.tensor_copy
        scopy = nc.scalar.copy

        banks = {"k": ps_k, "v": ps_vq, "q": ps_vq, "tp": ps_tp}

        def bank(tag):
            return banks[tag].tile([P, 4, P], F32, name="bk", tag=tag)

        b_rows = const.tile([24, P], BF16, name="b_rows")
        x_rows = x.rearrange("(z b) (g l) (i r) w -> l (b g) i z (r w)", z=2, l=2, r=16)
        w_view = W_qkv.rearrange("(s c p) k -> c p s k", s=3, c=NCHUNK, p=P)
        xn = [xpool.tile([P, 4096], BF16, name="xn%d" % h) for h in range(2)]
        wn = [wnat.tile([P, 3, 1024], BF16, name="wn", tag="wn") for c in range(NCHUNK)]

        def load_x(l, q, queue):
            queue.dma_start(out=xn[l][q : q + 125 : 4, :], in_=x_rows[l][q])

        def load_kv(c):
            nc.sync.dma_start(out=wn[c][:, 1:3, :], in_=w_view[c][:, 1:3, :])

        def load_q(c):
            nc.sync.dma_start(out=wn[c][:, 0:1, :], in_=w_view[c][:, 0:1, :])

        for l in range(2):
            for q in (2, 3):
                load_x(l, q, nc.scalar)
        nc.sync.dma_start(out=b_rows[:], in_=b_qkv.rearrange("(t p) -> t p", p=P))
        load_kv(0)
        for l in range(2):
            for q in (0, 1):
                load_x(l, q, nc.sync)
        load_kv(1)
        load_q(0)
        for c in range(2, NCHUNK):
            load_kv(c)
            load_q(c - 1)
        load_q(NCHUNK - 1)

        ident = const.tile([P, P], F32, name="ident")
        make_identity(nc, ident[:])
        pidx = const.tile([P, 1], I32, name="pidx")
        nc.gpsimd.iota(pidx[:], pattern=[[0, 1]], base=0, channel_multiplier=1)
        ones = const.tile([P, P], F32, name="ones")
        nc.gpsimd.memset(ones[:], 1.0)
        s_i = const.tile([P, 1], I32, name="s_i")
        nc.vector.tensor_single_scalar(out=s_i[:], in_=pidx[:], scalar=15, op=ALU.bitwise_and)
        r_i = const.tile([P, 1], I32, name="r_i")
        nc.vector.tensor_single_scalar(out=r_i[:], in_=pidx[:], scalar=4, op=ALU.logical_shift_right)
        s_f = const.tile([P, 1], F32, name="s_f")
        vcopy(out=s_f[:], in_=s_i[:])
        r_f = const.tile([P, 1], F32, name="r_f")
        vcopy(out=r_f[:], in_=r_i[:])
        tab = const.tile([P, 8], F32, name="tab")
        nc.scalar.activation(out=tab[:, 0:1], in_=s_f[:], func=ACT.Exp, scale=0.125, bias=-1.875)
        nc.scalar.activation(out=tab[:, 1:2], in_=s_f[:], func=ACT.Exp, scale=-0.125)
        for rh in range(2):
            nc.scalar.activation(
                out=tab[:, 2 + rh : 3 + rh], in_=r_f[:], func=ACT.Exp, scale=0.125, bias=(8.0 * rh - 15.0) / 8.0
            )
            nc.scalar.activation(
                out=tab[:, 4 + rh : 5 + rh], in_=r_f[:], func=ACT.Exp, scale=-0.125, bias=-1.0 * rh
            )
        b_rows_f = const.tile([P, P], F32, name="b_rows_f")
        nc.vector.memset(b_rows_f[:], 0.0)
        vcopy(out=b_rows_f[0:24, :], in_=b_rows[:])
        b_ps = bank("tp")
        nc.tensor.transpose(out=b_ps[:, 0, :], in_=b_rows_f[:], identity=ident[:])
        bias = const.tile([P, 24], F32, name="bias")
        vcopy(out=bias[:], in_=b_ps[:, 0, 0:24])
        cb = const.tile([P, NCHUNK], F32, name="cb")
        nc.vector.tensor_mul(out=cb[:], in0=bias[:, 8:16], in1=bias[:, 16:24])
        hs = const.tile([P, 1], F32, name="hs")
        nc.vector.scalar_tensor_tensor(
            out=hs[:], in0=tab[:, 0:1], scalar=1.0, in1=tab[:, 1:2], op0=ALU.add, op1=ALU.add
        )
        cbh = const.tile([P, NCHUNK], F32, name="cbh")
        nc.vector.tensor_scalar_mul(out=cbh[:], in0=cb[:], scalar1=hs[:, 0:1])

        xr = xpool.tile([P, 4096], F32, name="xr")
        xg = xpool.tile([P, 8192], BF16, name="xg", align_bytes=64)
        xc = xpool.tile([P, 2048], U32, name="xc", align_bytes=64)
        xs = xpool.tile([P, 2048], U8, name="xs", align_bytes=64)

        def x_reorder(l, j0, j1, copy):
            src = xn[l][:].bitcast(F32).rearrange("p (r j s u) -> p j r s u", r=16, j=16, s=4, u=2)
            dst = xr[:].rearrange("p (j u l r s) -> p l j r s u", j=16, u=2, l=2, r=16, s=4)
            copy(out=dst[:, l, j0:j1], in_=src[:, j0:j1])

        def x_bank(jp, tag, copy):
            t = bank(tag)
            for ju in range(4):
                c0 = (4 * jp + ju) * P
                nc.tensor.transpose(out=t[:, ju, :], in_=xr[:, c0 : c0 + P], identity=ident[:])
            src = t[:].rearrange("p (j u) (n g) -> p g j n u", j=2, u=2, n=YJ, g=2)
            dst = xg[:].bitcast(F32).rearrange("p (h g q j n u) -> p h q g j n u", h=2, g=2, q=4, j=2, n=YJ, u=2)
            copy(out=dst[:, jp // 4, jp % 4], in_=src)

        def x_quant(half, g):
            b = 2 * half + g
            nc.vector.quantize_mx(
                out=xc[:, b * BANK : (b + 1) * BANK].bitcast(FP8X4),
                scales=xs[:, b * BANK : (b + 1) * BANK],
                in_=xg[:, 4 * b * BANK : 4 * (b + 1) * BANK],
            )

        wg_kv = {}
        wg_q = {}
        wc_kv = {}
        ws_kv = {}
        wc_q = {}
        ws_q = {}

        def w_bank(c, section, dst):
            wt = bank("tp")
            words = wn[c][:, section, :].bitcast(F32)
            for chn in range(4):
                g, u = divmod(chn, 2)
                nc.tensor.transpose(
                    out=wt[:, chn, :], in_=words[:, 256 * g + u : 256 * (g + 1) : 2], identity=ident[:]
                )
            scopy(out=dst, in_=wt[:].rearrange("p (g u) o -> p g o u", g=2, u=2))

        def w_transpose_kv(c, t):
            if t == 0:
                wg_kv[c] = work2.tile([P, 2048], BF16, name="wgkv", tag="wgkv", align_bytes=64)
            v = wg_kv[c][:].bitcast(F32).rearrange("p (t g o u) -> p t g o u", t=2, g=2, o=P, u=2)
            w_bank(c, 1 + t, v[:, t])

        def w_transpose_q(c):
            wg_q[c] = work2.tile([P, 1024], BF16, name="wgq", tag="wgq", align_bytes=64)
            w_bank(c, 0, wg_q[c][:].bitcast(F32).rearrange("p (g o u) -> p g o u", g=2, o=P, u=2))

        def w_quant_kv(c):
            wc_kv[c] = work3.tile([P, 512], U32, name="wckv", tag="wckv", align_bytes=64)
            ws_kv[c] = work3.tile([P, 512], U8, name="wskv", tag="wskv", align_bytes=64)
            nc.vector.quantize_mx(out=wc_kv[c][:].bitcast(FP8X4), scales=ws_kv[c][:], in_=wg_kv[c][:])

        def w_quant_q(c):
            wc_q[c] = work3.tile([P, 256], U32, name="wcq", tag="wcq", align_bytes=64)
            ws_q[c] = work3.tile([P, 256], U8, name="wsq", tag="wsq", align_bytes=64)
            nc.vector.quantize_mx(out=wc_q[c][:].bitcast(FP8X4), scales=ws_q[c][:], in_=wg_q[c][:])

        def mx(codes, scales, first, half, tag):
            acc = banks[tag].tile([P, BANK], F32, name="acc", tag=tag)
            for g in range(2):
                pats = slice((2 * half + g) * BANK, (2 * half + g + 1) * BANK)
                cols = slice(first + g * P, first + (g + 1) * P)
                nc.tensor.matmul_mx(
                    out=acc[:],
                    lhsT=codes[:, cols].bitcast(FP8X4),
                    lhsT_scale=scales[:, cols],
                    rhs=xc[:, pats].bitcast(FP8X4),
                    rhs_scale=xs[:, pats],
                    start=(g == 0),
                    stop=(g == 1),
                )
            return acc

        ks = {}
        v_ps = {}
        q_ps = {}
        kv = {}
        tt = {}
        pt = {}
        qt = {}
        zt = {}
        ut = {}
        o_tiles = {}
        os_tiles = {}

        def borders(c):
            kv[c] = work2.tile([P, 18, YJ], F32, name="kv", tag="kv")
            nc.scalar.activation(
                out=kv[c][:, 0:18:17, :],
                in_=ones[:].rearrange("p (a y) -> p a y", a=2),
                func=ACT.Copy,
                scale=cb[:, c : c + 1],
            )
            tt[c] = work3.tile([P, 16, TROW], F32, name="tt", tag="tt")
            nc.scalar.activation(
                out=tt[c][:].rearrange("p j (l f) -> p j l f", f=4)[:, :, 1:19:17, :],
                in_=ones[:].rearrange("p (j l f) -> p j l f", j=16, l=2, f=4),
                func=ACT.Copy,
                scale=cbh[:, c : c + 1],
            )

        def front(c, half):
            if half == 0:
                ks[c] = work2.tile([P, NPATCH], F32, name="ks", tag="ks")
            if half == 1:
                v_ps[(c, half)] = mx(wc_kv[c], ws_kv[c], 256, half, "v")
            k_ps = mx(wc_kv[c], ws_kv[c], 0, half, "k")
            if half == 0:
                v_ps[(c, half)] = mx(wc_kv[c], ws_kv[c], 256, half, "v")
            nc.scalar.activation(
                out=ks[c][:, half * BANK : (half + 1) * BANK], in_=k_ps[:], func=ACT.Identity,
                bias=bias[:, 8 + c : 9 + c], scale=1.0,
            )

        def mx_q(c, half):
            q_ps[(c, half)] = mx(wc_q[c], ws_q[c], 0, half, "q" if c < NCHUNK - 1 else "v")

        def stt(o, a, s, b, op0, op1):
            nc.vector.scalar_tensor_tensor(out=o, in0=a, scalar=s, in1=b, op0=op0, op1=op1)

        def st_k(c, half):
            flat = kv[c][:].rearrange("p a y -> p (a y)")
            stt(
                flat[:, YJ + half * BANK : YJ + (half + 1) * BANK], v_ps[(c, half)][:], bias[:, 16 + c : 17 + c],
                ks[c][:, half * BANK : (half + 1) * BANK], ALU.add, ALU.mult,
            )

        def st_h1(c):
            flat = kv[c][:].rearrange("p a y -> p (a y)")
            pt[c] = work1.tile([P, 16, YJ], F32, name="pt", tag="pt")
            stt(
                pt[c][:].rearrange("p j y -> p (j y)"), flat[:, 0:NPATCH], tab[:, 0:1], flat[:, YJ : YJ + NPATCH],
                ALU.mult, ALU.add,
            )

        def st_h2(c):
            stt(tt[c][:, :, 8:72], kv[c][:, 2:18, :], tab[:, 1:2], pt[c][:], ALU.mult, ALU.add)

        def st_v1(c):
            rh = c % 2
            qt[c] = work2.tile([P, 16, YJ], F32, name="qt", tag="qt")
            ut[c] = work2.tile([P, 16, YJ], F32, name="ut", tag="ut")
            stt(qt[c][:], tt[c][:, :, 4:68], tab[:, 2 + rh : 3 + rh], tt[c][:, :, 8:72], ALU.mult, ALU.add)

        def gp_rows(c):
            return 6 if c == 0 else 8 if c == NCHUNK - 1 else GP_J

        def st_z(c):
            rh = c % 2
            nj = gp_rows(c)
            zt[c] = work2.tile([P, GP_J, YJ], F32, name="zt", tag="zt")
            nc.scalar.activation(
                out=zt[c][:, 0:nj, :], in_=tt[c][:, 0:nj, 12:76], func=ACT.Copy, scale=tab[:, 4 + rh : 5 + rh]
            )

        def st_g(c):
            nj = gp_rows(c)
            nc.gpsimd.tensor_tensor(
                out=ut[c][:, 0:nj, :], in0=qt[c][:, 0:nj, :], in1=zt[c][:, 0:nj, :], op=ALU.add
            )

        def st_v2(c, js):
            rh = c % 2
            stt(ut[c][:, js, :], tt[c][:, js, 12:76], tab[:, 4 + rh : 5 + rh], qt[c][:, js, :], ALU.mult, ALU.add)

        def st_f(c, half):
            ch = c // 2
            rh = c % 2
            if ch not in o_tiles:
                o_tiles[ch] = work2.tile([P, 2048], F32, name="ot", tag="ot")
            o_v = o_tiles[ch][:].rearrange("p (n a b) -> p n a b", a=2, b=4)
            stt(
                o_v[:, half * P : (half + 1) * P, rh, :],
                q_ps[(c, half)][:].rearrange("p (n b) -> p n b", b=4),
                bias[:, c : c + 1],
                ut[c][:].rearrange("p j (i b) -> p (j i) b", b=4)[:, half * P : (half + 1) * P, :],
                ALU.add, ALU.mult,
            )

        def out_bank(ch, q, copy, tag):
            if ch not in os_tiles:
                os_tiles[ch] = work2.tile([P, 8, 16, 16], F32, name="os_t", tag="os")
            tp = bank(tag)
            for jj in range(4):
                j = 4 * q + jj
                nc.tensor.transpose(out=tp[:, jj, :], in_=o_tiles[ch][:, j * P : (j + 1) * P], identity=ident[:])
            copy(
                out=os_tiles[ch][:, :, 4 * q : 4 * q + 4, :],
                in_=tp[:].rearrange("p j (r s) -> p r j s", r=8, s=16),
            )

        def out_store(ch):
            os_flat = os_tiles[ch][:].rearrange("p r j s -> p (r j s)")
            for b in range(4):
                nc.sync.dma_start(
                    out=out[b, ch].rearrange("(m r) w -> m (r w)", r=8), in_=os_flat[b : b + 125 : 4, :]
                )

        def out_store_half(ch, half):
            px = slice(half * 128, (half + 1) * 128)
            for b in range(4):
                nc.sync.dma_start(
                    out=out[b, ch].rearrange("(m r) w -> m r w", r=8)[:, :, px],
                    in_=os_tiles[ch][b : b + 125 : 4, :, 8 * half : 8 * half + 8, :],
                )

        def warm_up(n):
            t = bank("q")
            data = xr[:].bitcast(BF16).rearrange("p (m l w) -> p l m w", m=32, l=2, w=P)[:, 0]
            for i in range(n):
                nc.tensor.matmul(out=t[:], lhsT=data[:, 0, :], rhs=data[:, 0:4, :], start=True, stop=True)

        borders(0)
        w_transpose_kv(0, 0)
        w_transpose_kv(0, 1)
        for l in range(2):
            x_reorder(l, 0, 10, vcopy)
            x_reorder(l, 10, 16, scopy)
            if l == 0:
                w_quant_kv(0)
                warm_up(WARM)
        x_bank(0, "v", vcopy)
        x_bank(1, "v", scopy)
        x_bank(2, "q", vcopy)
        x_bank(3, "q", scopy)
        x_bank(4, "k", scopy)
        x_quant(0, 0)
        x_quant(0, 1)
        x_bank(5, "tp", scopy)
        x_bank(6, "tp", vcopy)
        x_bank(7, "tp", scopy)
        front(0, 0)
        x_quant(1, 0)
        x_quant(1, 1)
        w_transpose_kv(1, 0)
        w_transpose_kv(1, 1)
        front(0, 1)
        w_transpose_kv(2, 0)

        last = NCHUNK - 1
        for p in range(NCHUNK):
            st_k(p, 0)
            if p == 0:
                w_quant_kv(1)
            st_k(p, 1)
            if p == 1:
                w_quant_q(0)
            if p >= 1:
                st_g(p - 1)
            if p >= 2:
                st_f(p - 2, 0)
                st_f(p - 2, 1)
            if p == 0:
                st_h1(0)
            if p + 1 <= last:
                borders(p + 1)
                front(p + 1, 0)
                front(p + 1, 1)
            if p == 0:
                w_transpose_kv(2, 1)
                w_transpose_q(0)
            elif p + 2 <= last:
                w_transpose_kv(p + 2, 0)
                w_transpose_kv(p + 2, 1)
            if p >= 1:
                mx_q(p - 1, 0)
                mx_q(p - 1, 1)
                st_h1(p)
                w_quant_q(p)
            st_h2(p)
            if p >= 1:
                st_v2(p - 1, slice(gp_rows(p - 1), 16))
            st_z(p)
            if p + 1 <= last:
                w_transpose_q(p + 1)
            if p >= 3:
                ch, second = divmod(p - 3, 2)
                out_bank(ch, 2 * second, scopy, "tp")
                out_bank(ch, 2 * second + 1, scopy, "tp")
                if p == last:
                    mx_q(last, 0)
                    mx_q(last, 1)
                    out_bank(ch, 2, scopy, "tp")
                    out_bank(ch, 3, scopy, "tp")
                if second or p == last:
                    out_store(ch)
            st_v1(p)
            if p + 2 <= last:
                w_quant_kv(p + 2)
        st_g(last)
        st_f(last - 1, 0)
        st_f(last - 1, 1)
        st_v2(last, slice(8, 16))
        st_f(last, 0)
        out_bank(3, 0, scopy, "tp")
        out_bank(3, 1, scopy, "tp")
        out_store_half(3, 0)
        st_f(last, 1)
        out_bank(3, 2, vcopy, "q")
        out_bank(3, 3, scopy, "q")
        out_store_half(3, 1)
